import numpy as np
import ml_dtypes


def mxq(x, axis, fmt="e4m3"):
    dtype, down = {"e4m3": (ml_dtypes.float8_e4m3fn, 7), "e5m2": (ml_dtypes.float8_e5m2, 14)}[fmt]
    v = np.moveaxis(np.asarray(x, np.float32).astype(ml_dtypes.bfloat16).astype(np.float64), axis, -1)
    blocks = v.reshape(v.shape[:-1] + (-1, 32))
    amax = np.abs(blocks).max(-1, keepdims=True)
    byte = np.maximum(np.where(amax > 0, np.frexp(amax)[1] - 1 + 127, 0) - down, 1)
    scale = np.exp2(byte - 127.0)
    codes = (blocks / scale).astype(np.float32).astype(dtype).astype(np.float64)
    return np.moveaxis((codes * scale).reshape(v.shape), -1, axis)


WIDE = False


def mx_kscale(k):
    if not WIDE:
        return np.ones(k)
    levels = np.array([18, -18])
    if k % 512:
        return np.exp2(np.random.permutation(np.resize(levels, k // 32))).repeat(32)
    a = np.empty((k // 512, 16))
    for p in range(k // 512):
        a[p, :8] = np.random.permutation(np.resize(levels, 8))
        for g in range(8):
            far = levels[np.abs(levels - a[p, g]) >= 10]
            a[p, g + 8] = far[np.random.randint(len(far))]
    return np.exp2(a.ravel()).repeat(32)


BF16 = ml_dtypes.bfloat16


def bf(x):
    return np.asarray(x, np.float32).astype(BF16)


def f64(x):
    return np.asarray(x).astype(np.float64)


B, S, D_MODEL = 1, 1024, 1024


def relu(v):
    return np.maximum(v, 0.0)


def setup_inputs():
    s = mx_kscale(S)[:, None]
    u = mx_kscale(D_MODEL)
    v = mx_kscale(S)[:, None]
    qp0 = bf(np.random.standard_normal((B, S, D_MODEL)) * 0.4)
    kp0 = bf(np.random.standard_normal((B, S, D_MODEL)) * 0.4)
    vp0 = bf(np.random.standard_normal((B, S, D_MODEL)) * 0.25)
    mask = bf(np.random.standard_normal((1, S, S)) * 0.1)
    g = bf(np.random.standard_normal((B, S, D_MODEL)) * np.exp2(np.random.randint(-6, 1, (B, S, 1))) * 4.0 / s * u)
    z1 = f64(qp0) @ f64(kp0).transpose(0, 2, 1)
    z2 = (relu(z1) / np.sqrt(D_MODEL) + f64(mask)) @ f64(vp0)
    return {"qp": bf(f64(qp0) * s), "kp": bf(f64(kp0) / v), "vp": bf(f64(vp0) * v / u), "mask": mask,
            "z1": np.asarray(z1, np.float32), "z2": np.asarray(z2, np.float32), "grad_out": g}


def reference(qp, kp, vp, mask, z1, z2, grad_out):
    dz2 = f64(grad_out) * (f64(z2) > 0.0)
    dl = mxq(dz2, 2, "e5m2") @ mxq(f64(vp), 2, "e4m3").transpose(0, 2, 1)
    dz1 = dl * (f64(z1) > 0.0) / np.sqrt(D_MODEL)
    dq = mxq(dz1, 2, "e5m2") @ mxq(f64(kp), 1, "e4m3")
    dk = mxq(dz1, 1, "e5m2").transpose(0, 2, 1) @ mxq(f64(qp), 1, "e4m3")
    return dq, dk

@@ -1,0 +1,338 @@
+from contextlib import ExitStack
+
+import concourse.mybir as mybir
+from concourse.masks import make_identity
+
+S = 1024
+D = 1024
+FLOPS = 3 * 2 * S * S * D
+BYTES = 4 * S * D * 2 + 2 * S * D * 4 + 2 * S * D * 4
+
+F32 = mybir.dt.float32
+BF16 = mybir.dt.bfloat16
+U32 = mybir.dt.uint32
+U8 = mybir.dt.uint8
+E4 = mybir.dt.float8_e4m3fn_x4
+E5 = mybir.dt.float8_e5m2_x4
+ALU = mybir.AluOpType
+COPY = mybir.ActivationFunctionType.Copy
+
+P = 128
+N = 512
+SCALE = 1.0 / 32.0
+
+
+def tile_scaledconvolutionaldotproduct_pa_v_kernel(tc, qp, kp, vp, mask, z1, z2, grad_out, out_0, out_1):
+    nc = tc.nc
+    qp, kp, vp, z1, z2, grad_out, out_0, out_1 = [a.flatten_outer_dims() for a in (qp, kp, vp, z1, z2, grad_out, out_0, out_1)]
+
+    def by_four(a):
+        return a.rearrange("(h p j) w -> h p j w", p=P, j=4)
+
+    qp4, kp4, z14, z24, g4, out04 = [by_four(a) for a in (qp, kp, z1, z2, grad_out, out_0)]
+    vp_rows = vp.rearrange("(b p) w -> p b w", p=P)
+
+    with ExitStack() as ctx:
+        keep = ctx.enter_context(tc.tile_pool(name="keep", bufs=1))
+        psum = ctx.enter_context(tc.psum_pool(name="psum", bufs=1))
+
+        ident = keep.tile([P, P], F32, name="ident")
+        make_identity(nc, ident[:])
+
+        def codes(name):
+            c = keep.tile([P, 2048], U32, name=name + "_codes", align_bytes=64)
+            s = keep.tile([P, 2048], U8, name=name + "_scales", align_bytes=64)
+            return c, s
+
+        v_c, v_s = codes("v")
+        k_c, k_s = codes("k")
+        q_c, q_s = codes("q")
+        t_c, t_s = codes("t")
+        d_c, d_s = codes("d")
+        r_c, r_s = codes("r")
+
+        def sb(shape, dt, tag):
+            return keep.tile(shape, dt, tag=tag, name=tag, align_bytes=64)
+
+        counters = {}
+
+        def rot(key, n):
+            i = counters.get(key, 0)
+            counters[key] = i + 1
+            return key + str(i % n)
+
+        def bank(group):
+            order = {"all": "01234567", "T": "01", "E": "234", "O": "567"}[group]
+            i = counters.get("bank" + group, 0)
+            counters["bank" + group] = i + 1
+            return psum.tile([P, N], F32, tag="bank" + order[i % len(order)], name="bank")
+
+        v_grp = {n: sb([P, 4096], BF16, "raw_z23" if n == 0 else "raw_z13") for n in range(2)}
+
+        raw = {}
+
+        def load(tile_ap, src):
+            nc.sync.dma_start(out=tile_ap, in_=src)
+
+        def load_v(i):
+            if i % 2 == 0:
+                raw["v", i // 2] = sb([P, 4, D], BF16, "raw_v" + str(i // 2))
+            load(raw["v", i // 2][:, 2 * (i % 2) : 2 * (i % 2) + 2, :], vp_rows[:, 2 * i : 2 * i + 2, :])
+
+        def load_g(i):
+            h, j = i // 2, 2 * (i % 2)
+            raw["g", i] = sb([P, 2, D], BF16, "raw_g" + str(i))
+            load(raw["g", i][:], g4[h, :, j : j + 2, :])
+
+        def load_z2(i):
+            h, j = i // 2, 2 * (i % 2)
+            raw["z2", i] = sb([P, 2, D], F32, "raw_z2" + str(i))
+            load(raw["z2", i][:], z24[h, :, j : j + 2, :])
+
+        def load_z1(h, n):
+            raw["z1", h, n] = sb([P, 4, N], F32, "raw_z1" + str(2 * h + n))
+            load(raw["z1", h, n][:], z14[h, :, :, n * N : (n + 1) * N])
+
+        def load_k(h):
+            raw["k", h] = sb([P, 4, D], BF16, "raw_k" + str(h))
+            load(raw["k", h][:], kp4[h])
+
+        def load_q(h):
+            raw["q", h] = sb([P, 4, D], BF16, "raw_v" + str(h))
+            load(raw["q", h][:], qp4[h])
+
+        def copy_out(eng, out, in_):
+            if eng == "S":
+                nc.scalar.copy(out=out, in_=in_)
+            else:
+                nc.vector.tensor_copy(out=out, in_=in_)
+
+        def transpose_words(group, blocks):
+            b = bank(group)
+            for i, w in enumerate(blocks):
+                nc.tensor.transpose(b[:, i * P : (i + 1) * P], w, ident[:])
+            return b
+
+        def words(tile2d, start):
+            w = tile2d.bitcast(F32)
+            return [w[:, start + u : start + 256 : 2] for u in (0, 1)]
+
+
+        def v_block(b, eng):
+            n, i = b // 4, b % 4
+            row = raw["v", n][:, i, :]
+            bk = transpose_words("all", words(row, 0) + words(row, 256))
+            copy_out(
+                eng,
+                v_grp[n][:].bitcast(F32).rearrange("p (g r u) -> p g r u", g=2, u=2)[:, :, i * P : (i + 1) * P, :],
+                bk[:].rearrange("p (g u r) -> p g r u", g=2, u=2),
+            )
+
+        def quant(out_c, out_s, dt, grp, at, width):
+            nc.vector.quantize_mx(out=out_c[:, at : at + width].bitcast(dt), scales=out_s[:, at : at + width], in_=grp)
+
+        def v_quant(n):
+            for g in range(2):
+                quant(v_c, v_s, E4, v_grp[n][:, g * 2048 : (g + 1) * 2048], (2 * n + g) * N, N)
+
+        dz2 = {}
+
+        def mask_g(b):
+            i, j = b // 2, b % 2
+            dz2[b] = sb([P, D], BF16, rot("dz2_", 3))
+            nc.vector.scalar_tensor_tensor(
+                out=dz2[b][:], in0=raw["z2", i][:, j, :], scalar=0.0, in1=raw["g", i][:, j, :], op0=ALU.is_gt, op1=ALU.mult
+            )
+
+        def dz2_t(b):
+            bk = transpose_words("T", words(dz2[b][:], 0) + words(dz2[b][:], 256))
+            grp = sb([P, 1024], BF16, rot("tg", 3))
+            copy_out(
+                "S",
+                grp[:].bitcast(F32).rearrange("p (g r u) -> p g r u", g=2, u=2),
+                bk[:].rearrange("p (g u r) -> p g r u", g=2, u=2),
+            )
+            quant(t_c, t_s, E5, grp[:], b * 256, 256)
+
+        dl = {}
+
+        def dl_mm(b, n):
+            bk = bank("E")
+            for g in range(2):
+                nc.tensor.matmul_mx(
+                    out=bk[:],
+                    lhsT=t_c[:, b * 256 + g * P : b * 256 + (g + 1) * P].bitcast(E5),
+                    lhsT_scale=t_s[:, b * 256 + g * P : b * 256 + (g + 1) * P],
+                    rhs=v_c[:, (2 * n + g) * N : (2 * n + g + 1) * N].bitcast(E4),
+                    rhs_scale=v_s[:, (2 * n + g) * N : (2 * n + g + 1) * N],
+                    start=(g == 0),
+                    stop=(g == 1),
+                )
+            dl[b, n] = bk
+
+        dz1 = {}
+
+        def mask_dl(b, n):
+            h, j = b // 4, b % 4
+            if j == 0:
+                dz1[h, n] = sb([P, 4 * N], BF16, rot("dz1_", 3))
+            nc.vector.scalar_tensor_tensor(
+                out=dz1[h, n][:, j * N : (j + 1) * N], in0=raw["z1", h, n][:, j, :], scalar=0.0, in1=dl[b, n][:], op0=ALU.is_gt, op1=ALU.mult
+            )
+
+        def dz1_t(pair, n):
+            h, j = pair // 2, 2 * (pair % 2)
+            bk = transpose_words("T", words(dz1[h, n][:], j * 256) + words(dz1[h, n][:], (j + 1) * 256))
+            grp = sb([P, 1024], BF16, rot("dg", 3))
+            copy_out(
+                "S",
+                grp[:].bitcast(F32).rearrange("p (g r u) -> p g r u", g=2, u=2),
+                bk[:].rearrange("p (g u r) -> p g r u", g=2, u=2),
+            )
+            quant(d_c, d_s, E5, grp[:], n * 1024 + pair * 256, 256)
+
+        grp4 = {}
+
+        def interleave(eng, key, src, piece):
+            if piece % 2 == 0:
+                grp4[key] = sb([P, 2048], BF16, rot("grp", 5))
+            o = (piece % 2) * 1024
+            copy_out(
+                eng,
+                grp4[key][:, o : o + 1024].rearrange("p (c i t) -> p c t i", i=4, t=4),
+                src[:, :, piece * 256 : (piece + 1) * 256].rearrange("p t (c i) -> p c t i", i=4),
+            )
+
+        def kq_half(name, h, half, engs):
+            c, s = (k_c, k_s) if name == "k" else (q_c, q_s)
+            for i in range(2):
+                interleave(engs[i], (name, h, half), raw[name, h], 2 * half + i)
+            quant(c, s, E4, grp4[name, h, half][:], h * 1024 + half * N, N)
+
+        def r_quad(h, n, engs):
+            src = dz1[h, n][:].rearrange("p (t c) -> p t c", t=4)
+            for i in range(2):
+                interleave(engs[i], ("r", h, n), src, i)
+            quant(r_c, r_s, E5, grp4["r", h, n][:], h * 1024 + n * N, N)
+
+        def scaled_out(eng, out, in_):
+            if eng == "S":
+                nc.scalar.activation(out=out, in_=in_, func=COPY, scale=SCALE)
+            else:
+                nc.vector.tensor_scalar(out=out, in0=in_, scalar1=SCALE, scalar2=None, op0=ALU.mult)
+
+        o0 = {}
+
+        def out0_block(b, engs, group="O"):
+            i, j = b // 2, b % 2
+            if j == 0:
+                o0[i] = sb([P, 2, D], F32, "raw_z2" + str(i))
+            for f in range(2):
+                bk = bank(group)
+                for g in range(2):
+                    nc.tensor.matmul_mx(
+                        out=bk[:],
+                        lhsT=d_c[:, g * 1024 + b * P : g * 1024 + (b + 1) * P].bitcast(E5),
+                        lhsT_scale=d_s[:, g * 1024 + b * P : g * 1024 + (b + 1) * P],
+                        rhs=k_c[:, g * 1024 + f * N : g * 1024 + (f + 1) * N].bitcast(E4),
+                        rhs_scale=k_s[:, g * 1024 + f * N : g * 1024 + (f + 1) * N],
+                        start=(g == 0),
+                        stop=(g == 1),
+                    )
+                scaled_out(engs[f], o0[i][:, j, f * N : (f + 1) * N], bk[:])
+            if j == 1:
+                nc.sync.dma_start(out=out04[i // 2, :, 2 * (i % 2) : 2 * (i % 2) + 2, :], in_=o0[i][:])
+
+        o1 = {}
+
+        def out1_block(m, engs, group):
+            if m % 2 == 0:
+                o1[m // 2] = sb([P, 2, D], F32, "raw_z1" + str(m // 2))
+            for f in range(2):
+                bk = bank(group)
+                for g in range(2):
+                    nc.tensor.matmul_mx(
+                        out=bk[:],
+                        lhsT=r_c[:, g * 1024 + m * P : g * 1024 + (m + 1) * P].bitcast(E5),
+                        lhsT_scale=r_s[:, g * 1024 + m * P : g * 1024 + (m + 1) * P],
+                        rhs=q_c[:, g * 1024 + f * N : g * 1024 + (f + 1) * N].bitcast(E4),
+                        rhs_scale=q_s[:, g * 1024 + f * N : g * 1024 + (f + 1) * N],
+                        start=(g == 0),
+                        stop=(g == 1),
+                    )
+                scaled_out(engs[f], o1[m // 2][:, m % 2, f * N : (f + 1) * N], bk[:])
+            nc.sync.dma_start(out=out_1[m * P : (m + 1) * P, :], in_=o1[m // 2][:, m % 2, :])
+
+        load_v(0)
+        load_v(1)
+        load_g(0)
+        load_z2(0)
+        load_k(0)
+        load_z1(0, 0)
+        load_g(1)
+        load_z2(1)
+        load_v(2)
+        load_v(3)
+        load_k(1)
+        load_z1(0, 1)
+
+        for b in range(4):
+            v_block(b, "S")
+        v_quant(0)
+
+        def half_n0(h, extra):
+            for b in range(4 * h, 4 * h + 4):
+                mask_g(b)
+                dz2_t(b)
+                dl_mm(b, 0)
+                mask_dl(b, 0)
+                if b % 2:
+                    dz1_t(b // 2, 0)
+                extra(b)
+
+        def extra0(b):
+            if b < 2:
+                kq_half("k", 0, b, "VS")
+            else:
+                for i in range(2):
+                    v_block(2 * b + i, "S")
+
+        half_n0(0, extra0)
+        load_g(2)
+        load_z2(2)
+        load_z1(1, 0)
+        load_g(3)
+        v_quant(1)
+        load_z2(3)
+        load_q(0)
+        load_q(1)
+        load_z1(1, 1)
+        for b in range(4):
+            dl_mm(b, 1)
+            mask_dl(b, 1)
+            if b % 2:
+                dz1_t(b // 2, 1)
+            if b < 2:
+                kq_half("k", 1, b, "VS")
+        r_quad(0, 0, "VS")
+        r_quad(0, 1, "VS")
+
+        def extra1(b):
+            out0_block(b - 4, "SS")
+
+        half_n0(1, extra1)
+        for h in range(2):
+            for half in range(2):
+                kq_half("q", h, half, "VS")
+        r_quad(1, 0, "VS")
+        for b in range(4, 8):
+            dl_mm(b, 1)
+            mask_dl(b, 1)
+            if b % 2:
+                dz1_t(b // 2, 1)
+            out1_block(b - 4, "SV", "O")
+        r_quad(1, 1, "VS")
+        for b in range(4, 8):
+            out0_block(b, "SV", "O")
+        for m in range(4, 8):
+            out1_block(m, "SV", "all")

@@ -21,6 +21,21 @@ P = 128
 N = 512
 SCALE = 1.0 / 32.0
 
+ORDER = (
+    "vp0 vp2 vp3 vT0 vp1 vT1 vC0:V vT5 g1 vC1:S vT4 vC5:V vT6 z21 vC4:S vT7 vC6:V vT3 vC7:S vT2 vC3:S vQ10:V g0 "
+    "vC2:V z20 vQ00:V vQ01:V A2:V kp0 vQ11:V B2 A3:V C2:S D2:V B3 A0:V z100 E20 C3:S E21 A1:V B0 D3:V kp1 B1 C0:V "
+    "E30 kI000:V C1:S D0:V kI001:S D1:V F20:V E10 z101 kI011:S F30:V E00 kQ00:V kI010:S G10 F00:V E01 kI100:S "
+    "kI101:V g3 E31 F10:V E11 H10:S kQ01:V z23 kI110:S G00 kQ10:V F31:V H00:S F01:V kI111:S F21:V qp0 dI001:S F11:V "
+    "G11 I00:V dI000:S G01 kQ11:V A6:V H01:S z22 H11:S I01:V dI010:S B6 dQ00:V J01 I11:V C6:S qI011:V g2 J11 qI001:S "
+    "I10:V J10 D6:V z110 A7:V J31 qI000:S J30 K31:S dI011:V J00 K10:S qQ00:V J21 qI010:S J20 z111 A4:V E60 K00:S "
+    "A5:V B7 K21:S B4 C7:S qQ01:V qp1 B5 C4:S D7:V E61 F60:V C5:S E70 D4:V K01:S D5:V E40 K11:S F70:V E51 K30:S "
+    "F40:V E50 K20:S F51:V so0 E41 F50:V E71 F41:V dI100:S G20 F71:V G21 F61:V H20:S so1 G30 H21:S G31 I20:V qI110:S "
+    "I21:V H31:V J40 H30:S qI101:V J50 K40:S I30:V J41 I31:V K50:S dI101:V J51 K41:S J60 qI100:V K51:S J61 dQ10:V "
+    "qI111:S J71 qQ10:V J70 K60:V so2 K71:S O10 K61:V K70:S O20 qQ11:V dI111:S O00 P20:V O21 so3 dI110:V O31 P21:S "
+    "dQ01:V O30 P00:S dQ11:V O01 P30:S P31:V O11 sp2 P10:S O51 P01:V O71 P11:V sp3 P51:S O41 P71:S O40 sp0 P41:V O70 "
+    "P40:V O61 sp1 P70:V O60 P61:S O50 sp4 P60:S P50:V sp7 sp5 sp6 "
+).split()
+
 
 def tile_scaledconvolutionaldotproduct_pa_v_kernel(tc, qp, kp, vp, mask, z1, z2, grad_out, out_0, out_1):
     nc = tc.nc
@@ -54,52 +69,45 @@ def tile_scaledconvolutionaldotproduct_pa_v_kernel(tc, qp, kp, vp, mask, z1, z2,
         def sb(shape, dt, tag):
             return keep.tile(shape, dt, tag=tag, name=tag, align_bytes=64)
 
-        counters = {}
+        free_banks = ["bank" + str(i) for i in range(8)]
+        bank_of = {}
+        free_slots = {k: [k + str(i) for i in range(n)] for k, n in (("grp", 5), ("dz2_", 4), ("tg", 4), ("dg", 4), ("raw_g", 3))}
+        slot_of = {}
 
-        def rot(key, n):
-            i = counters.get(key, 0)
-            counters[key] = i + 1
-            return key + str(i % n)
+        def take(kind, key):
+            tag = free_slots[kind][0]
+            free_slots[kind].remove(tag)
+            slot_of[key] = (kind, tag)
+            return tag
 
-        def bank(group):
-            order = {"all": "01234567", "T": "01", "E": "234", "O": "567"}[group]
-            i = counters.get("bank" + group, 0)
-            counters["bank" + group] = i + 1
-            return psum.tile([P, N], F32, tag="bank" + order[i % len(order)], name="bank")
+        def give(key):
+            kind, tag = slot_of[key]
+            free_slots[kind].append(tag)
+
+        def bank(key):
+            tag = free_banks[0]
+            free_banks.remove(tag)
+            bank_of[key] = (psum.tile([P, N], F32, tag=tag, name="bank"), tag)
+            return bank_of[key][0]
+
+        def drain(key):
+            tile, tag = bank_of[key]
+            free_banks.append(tag)
+            return tile
 
         v_grp = {n: sb([P, 4096], BF16, "raw_z23" if n == 0 else "raw_z13") for n in range(2)}
-
         raw = {}
+        masked = []
+        dz2 = {}
+        tg = {}
+        dz1 = {}
+        dg = {}
+        grp4 = {}
+        o0 = {}
+        o1 = {}
 
-        def load(tile_ap, src):
-            nc.sync.dma_start(out=tile_ap, in_=src)
-
-        def load_v(i):
-            if i % 2 == 0:
-                raw["v", i // 2] = sb([P, 4, D], BF16, "raw_v" + str(i // 2))
-            load(raw["v", i // 2][:, 2 * (i % 2) : 2 * (i % 2) + 2, :], vp_rows[:, 2 * i : 2 * i + 2, :])
-
-        def load_g(i):
-            h, j = i // 2, 2 * (i % 2)
-            raw["g", i] = sb([P, 2, D], BF16, "raw_g" + str(i))
-            load(raw["g", i][:], g4[h, :, j : j + 2, :])
-
-        def load_z2(i):
-            h, j = i // 2, 2 * (i % 2)
-            raw["z2", i] = sb([P, 2, D], F32, "raw_z2" + str(i))
-            load(raw["z2", i][:], z24[h, :, j : j + 2, :])
-
-        def load_z1(h, n):
-            raw["z1", h, n] = sb([P, 4, N], F32, "raw_z1" + str(2 * h + n))
-            load(raw["z1", h, n][:], z14[h, :, :, n * N : (n + 1) * N])
-
-        def load_k(h):
-            raw["k", h] = sb([P, 4, D], BF16, "raw_k" + str(h))
-            load(raw["k", h][:], kp4[h])
-
-        def load_q(h):
-            raw["q", h] = sb([P, 4, D], BF16, "raw_v" + str(h))
-            load(raw["q", h][:], qp4[h])
+        def load(out, src):
+            nc.sync.dma_start(out=out, in_=src)
 
         def copy_out(eng, out, in_):
             if eng == "S":
@@ -107,232 +115,175 @@ def tile_scaledconvolutionaldotproduct_pa_v_kernel(tc, qp, kp, vp, mask, z1, z2,
             else:
                 nc.vector.tensor_copy(out=out, in_=in_)
 
-        def transpose_words(group, blocks):
-            b = bank(group)
-            for i, w in enumerate(blocks):
-                nc.tensor.transpose(b[:, i * P : (i + 1) * P], w, ident[:])
-            return b
-
-        def words(tile2d, start):
-            w = tile2d.bitcast(F32)
-            return [w[:, start + u : start + 256 : 2] for u in (0, 1)]
-
-
-        def v_block(b, eng):
-            n, i = b // 4, b % 4
-            row = raw["v", n][:, i, :]
-            bk = transpose_words("all", words(row, 0) + words(row, 256))
-            copy_out(
-                eng,
-                v_grp[n][:].bitcast(F32).rearrange("p (g r u) -> p g r u", g=2, u=2)[:, :, i * P : (i + 1) * P, :],
-                bk[:].rearrange("p (g u r) -> p g r u", g=2, u=2),
-            )
-
-        def quant(out_c, out_s, dt, grp, at, width):
-            nc.vector.quantize_mx(out=out_c[:, at : at + width].bitcast(dt), scales=out_s[:, at : at + width], in_=grp)
-
-        def v_quant(n):
-            for g in range(2):
-                quant(v_c, v_s, E4, v_grp[n][:, g * 2048 : (g + 1) * 2048], (2 * n + g) * N, N)
-
-        dz2 = {}
-
-        def mask_g(b):
-            i, j = b // 2, b % 2
-            dz2[b] = sb([P, D], BF16, rot("dz2_", 3))
-            nc.vector.scalar_tensor_tensor(
-                out=dz2[b][:], in0=raw["z2", i][:, j, :], scalar=0.0, in1=raw["g", i][:, j, :], op0=ALU.is_gt, op1=ALU.mult
-            )
-
-        def dz2_t(b):
-            bk = transpose_words("T", words(dz2[b][:], 0) + words(dz2[b][:], 256))
-            grp = sb([P, 1024], BF16, rot("tg", 3))
-            copy_out(
-                "S",
-                grp[:].bitcast(F32).rearrange("p (g r u) -> p g r u", g=2, u=2),
-                bk[:].rearrange("p (g u r) -> p g r u", g=2, u=2),
-            )
-            quant(t_c, t_s, E5, grp[:], b * 256, 256)
-
-        dl = {}
-
-        def dl_mm(b, n):
-            bk = bank("E")
-            for g in range(2):
-                nc.tensor.matmul_mx(
-                    out=bk[:],
-                    lhsT=t_c[:, b * 256 + g * P : b * 256 + (g + 1) * P].bitcast(E5),
-                    lhsT_scale=t_s[:, b * 256 + g * P : b * 256 + (g + 1) * P],
-                    rhs=v_c[:, (2 * n + g) * N : (2 * n + g + 1) * N].bitcast(E4),
-                    rhs_scale=v_s[:, (2 * n + g) * N : (2 * n + g + 1) * N],
-                    start=(g == 0),
-                    stop=(g == 1),
-                )
-            dl[b, n] = bk
-
-        dz1 = {}
-
-        def mask_dl(b, n):
-            h, j = b // 4, b % 4
-            if j == 0:
-                dz1[h, n] = sb([P, 4 * N], BF16, rot("dz1_", 3))
-            nc.vector.scalar_tensor_tensor(
-                out=dz1[h, n][:, j * N : (j + 1) * N], in0=raw["z1", h, n][:, j, :], scalar=0.0, in1=dl[b, n][:], op0=ALU.is_gt, op1=ALU.mult
-            )
-
-        def dz1_t(pair, n):
-            h, j = pair // 2, 2 * (pair % 2)
-            bk = transpose_words("T", words(dz1[h, n][:], j * 256) + words(dz1[h, n][:], (j + 1) * 256))
-            grp = sb([P, 1024], BF16, rot("dg", 3))
-            copy_out(
-                "S",
-                grp[:].bitcast(F32).rearrange("p (g r u) -> p g r u", g=2, u=2),
-                bk[:].rearrange("p (g u r) -> p g r u", g=2, u=2),
-            )
-            quant(d_c, d_s, E5, grp[:], n * 1024 + pair * 256, 256)
-
-        grp4 = {}
-
-        def interleave(eng, key, src, piece):
-            if piece % 2 == 0:
-                grp4[key] = sb([P, 2048], BF16, rot("grp", 5))
-            o = (piece % 2) * 1024
-            copy_out(
-                eng,
-                grp4[key][:, o : o + 1024].rearrange("p (c i t) -> p c t i", i=4, t=4),
-                src[:, :, piece * 256 : (piece + 1) * 256].rearrange("p t (c i) -> p c t i", i=4),
-            )
-
-        def kq_half(name, h, half, engs):
-            c, s = (k_c, k_s) if name == "k" else (q_c, q_s)
-            for i in range(2):
-                interleave(engs[i], (name, h, half), raw[name, h], 2 * half + i)
-            quant(c, s, E4, grp4[name, h, half][:], h * 1024 + half * N, N)
-
-        def r_quad(h, n, engs):
-            src = dz1[h, n][:].rearrange("p (t c) -> p t c", t=4)
-            for i in range(2):
-                interleave(engs[i], ("r", h, n), src, i)
-            quant(r_c, r_s, E5, grp4["r", h, n][:], h * 1024 + n * N, N)
-
         def scaled_out(eng, out, in_):
             if eng == "S":
                 nc.scalar.activation(out=out, in_=in_, func=COPY, scale=SCALE)
             else:
                 nc.vector.tensor_scalar(out=out, in0=in_, scalar1=SCALE, scalar2=None, op0=ALU.mult)
 
-        o0 = {}
+        def transpose_words(key, blocks):
+            b = bank(key)
+            for i, w in enumerate(blocks):
+                nc.tensor.transpose(b[:, i * P : (i + 1) * P], w, ident[:])
 
-        def out0_block(b, engs, group="O"):
-            i, j = b // 2, b % 2
-            if j == 0:
-                o0[i] = sb([P, 2, D], F32, "raw_z2" + str(i))
-            for f in range(2):
-                bk = bank(group)
-                for g in range(2):
-                    nc.tensor.matmul_mx(
-                        out=bk[:],
-                        lhsT=d_c[:, g * 1024 + b * P : g * 1024 + (b + 1) * P].bitcast(E5),
-                        lhsT_scale=d_s[:, g * 1024 + b * P : g * 1024 + (b + 1) * P],
-                        rhs=k_c[:, g * 1024 + f * N : g * 1024 + (f + 1) * N].bitcast(E4),
-                        rhs_scale=k_s[:, g * 1024 + f * N : g * 1024 + (f + 1) * N],
-                        start=(g == 0),
-                        stop=(g == 1),
-                    )
-                scaled_out(engs[f], o0[i][:, j, f * N : (f + 1) * N], bk[:])
-            if j == 1:
+        def words(tile2d, start):
+            w = tile2d.bitcast(F32)
+            return [w[:, start + u : start + 256 : 2] for u in (0, 1)]
+
+        def quant(out_c, out_s, dt, grp, at, width):
+            nc.vector.quantize_mx(out=out_c[:, at : at + width].bitcast(dt), scales=out_s[:, at : at + width], in_=grp)
+
+        def product(key, a_c, a_s, a_at, b_c, b_s, b_at):
+            bk = bank(key)
+            for g in range(2):
+                a = slice(a_at[g], a_at[g] + P)
+                b = slice(b_at[g], b_at[g] + N)
+                nc.tensor.matmul_mx(
+                    out=bk[:],
+                    lhsT=a_c[:, a].bitcast(E5),
+                    lhsT_scale=a_s[:, a],
+                    rhs=b_c[:, b].bitcast(E4),
+                    rhs_scale=b_s[:, b],
+                    start=(g == 0),
+                    stop=(g == 1),
+                )
+
+        def grouped(eng, out, bk):
+            copy_out(
+                eng,
+                out.bitcast(F32).rearrange("p (g r u) -> p g r u", g=2, u=2),
+                bk.rearrange("p (g u r) -> p g r u", g=2, u=2),
+            )
+
+        def op(name, eng):
+            c = name[0]
+            x = [int(ch) for ch in name if ch in "0123456789"]
+            k = "".join([ch for ch in name if ch not in "0123456789"])
+            if k == "vp":
+                i = x[0]
+                if ("v", i // 2) not in raw:
+                    raw["v", i // 2] = sb([P, 4, D], BF16, "raw_v" + str(i // 2))
+                load(raw["v", i // 2][:, 2 * (i % 2) : 2 * (i % 2) + 2, :], vp_rows[:, 2 * i : 2 * i + 2, :])
+            elif k == "g":
+                i = x[0]
+                raw["g", i] = sb([P, 2, D], BF16, take("raw_g", name))
+                load(raw["g", i][:], g4[i // 2, :, 2 * (i % 2) : 2 * (i % 2) + 2, :])
+            elif k == "z" and x[0] == 2:
+                i = x[1]
+                raw["z2", i] = sb([P, 2, D], F32, "raw_z2" + str(i))
+                load(raw["z2", i][:], z24[i // 2, :, 2 * (i % 2) : 2 * (i % 2) + 2, :])
+            elif k == "z":
+                h, n = x[1], x[2]
+                raw["z1", h, n] = sb([P, 4, N], F32, "raw_z1" + str(2 * h + n))
+                load(raw["z1", h, n][:], z14[h, :, :, n * N : (n + 1) * N])
+            elif k == "kp":
+                raw["k", x[0]] = sb([P, 4, D], BF16, "raw_k" + str(x[0]))
+                load(raw["k", x[0]][:], kp4[x[0]])
+            elif k == "qp":
+                raw["q", x[0]] = sb([P, 4, D], BF16, "raw_v" + str(x[0]))
+                load(raw["q", x[0]][:], qp4[x[0]])
+            elif k == "vT":
+                row = raw["v", x[0] // 4][:, x[0] % 4, :]
+                transpose_words(name, words(row, 0) + words(row, 256))
+            elif k == "vC":
+                n, i = x[0] // 4, x[0] % 4
+                copy_out(
+                    eng,
+                    v_grp[n][:].bitcast(F32).rearrange("p (g r u) -> p g r u", g=2, u=2)[:, :, i * P : (i + 1) * P, :],
+                    drain("vT" + str(x[0]))[:].rearrange("p (g u r) -> p g r u", g=2, u=2),
+                )
+            elif k == "vQ":
+                n, g = x
+                quant(v_c, v_s, E4, v_grp[n][:, g * 2048 : (g + 1) * 2048], (2 * n + g) * N, N)
+            elif k == "A":
+                b = x[0]
+                dz2[b] = sb([P, D], BF16, take("dz2_", name))
+                nc.vector.scalar_tensor_tensor(
+                    out=dz2[b][:], in0=raw["z2", b // 2][:, b % 2, :], scalar=0.0, in1=raw["g", b // 2][:, b % 2, :], op0=ALU.is_gt, op1=ALU.mult
+                )
+                masked.append(b)
+                if b ^ 1 in masked:
+                    give("g" + str(b // 2))
+            elif k == "B":
+                transpose_words(name, words(dz2[x[0]][:], 0) + words(dz2[x[0]][:], 256))
+                give("A" + str(x[0]))
+            elif k == "C":
+                b = x[0]
+                tg[b] = sb([P, 1024], BF16, take("tg", name))
+                grouped(eng, tg[b][:], drain("B" + str(b))[:])
+            elif k == "D":
+                quant(t_c, t_s, E5, tg[x[0]][:], x[0] * 256, 256)
+                give("C" + str(x[0]))
+            elif k == "E":
+                b, n = x
+                product(name, t_c, t_s, [b * 256 + g * P for g in range(2)], v_c, v_s, [(2 * n + g) * N for g in range(2)])
+            elif k == "F":
+                b, n = x
+                h, j = b // 4, b % 4
+                if (h, n) not in dz1:
+                    dz1[h, n] = sb([P, 4 * N], BF16, "dz1_" + str(2 * h + n))
+                nc.vector.scalar_tensor_tensor(
+                    out=dz1[h, n][:, j * N : (j + 1) * N],
+                    in0=raw["z1", h, n][:, j, :],
+                    scalar=0.0,
+                    in1=drain("E" + str(b) + str(n))[:],
+                    op0=ALU.is_gt,
+                    op1=ALU.mult,
+                )
+            elif k == "G":
+                p, n = x
+                h, j = p // 2, 2 * (p % 2)
+                transpose_words(name, words(dz1[h, n][:], j * 256) + words(dz1[h, n][:], (j + 1) * 256))
+            elif k == "H":
+                p, n = x
+                dg[p, n] = sb([P, 1024], BF16, take("dg", name))
+                grouped(eng, dg[p, n][:], drain("G" + str(p) + str(n))[:])
+            elif k == "I":
+                p, n = x
+                quant(d_c, d_s, E5, dg[p, n][:], n * 1024 + p * 256, 256)
+                give("H" + str(p) + str(n))
+            elif k in ("kI", "qI", "dI"):
+                h, f, i = x
+                if (c, h, f) not in grp4:
+                    grp4[c, h, f] = sb([P, 2048], BF16, take("grp", (c, h, f)))
+                if c == "d":
+                    src = dz1[h, f][:].rearrange("p (t c) -> p t c", t=4)[:, :, i * 256 : (i + 1) * 256]
+                else:
+                    src = raw[c, h][:, :, f * N + i * 256 : f * N + (i + 1) * 256]
+                copy_out(
+                    eng,
+                    grp4[c, h, f][:, i * 1024 : (i + 1) * 1024].rearrange("p (c i t) -> p c t i", i=4, t=4),
+                    src.rearrange("p t (c i) -> p c t i", i=4),
+                )
+            elif k in ("kQ", "qQ", "dQ"):
+                h, f = x
+                cc, ss, dt = {"k": (k_c, k_s, E4), "q": (q_c, q_s, E4), "d": (r_c, r_s, E5)}[c]
+                quant(cc, ss, dt, grp4[c, h, f][:], h * 1024 + f * N, N)
+                give((c, h, f))
+            elif k == "J":
+                b, f = x
+                product(name, d_c, d_s, [g * 1024 + b * P for g in range(2)], k_c, k_s, [g * 1024 + f * N for g in range(2)])
+            elif k == "K":
+                b, f = x
+                if b // 2 not in o0:
+                    o0[b // 2] = sb([P, 2, D], F32, "raw_z2" + str(b // 2))
+                scaled_out(eng, o0[b // 2][:, b % 2, f * N : (f + 1) * N], drain("J" + str(b) + str(f))[:])
+            elif k == "O":
+                m, f = x
+                product(name, r_c, r_s, [g * 1024 + m * P for g in range(2)], q_c, q_s, [g * 1024 + f * N for g in range(2)])
+            elif k == "P":
+                m, f = x
+                if m // 2 not in o1:
+                    o1[m // 2] = sb([P, 2, D], F32, "raw_z1" + str(m // 2))
+                scaled_out(eng, o1[m // 2][:, m % 2, f * N : (f + 1) * N], drain("O" + str(m) + str(f))[:])
+            elif k == "so":
+                i = x[0]
                 nc.sync.dma_start(out=out04[i // 2, :, 2 * (i % 2) : 2 * (i % 2) + 2, :], in_=o0[i][:])
-
-        o1 = {}
-
-        def out1_block(m, engs, group):
-            if m % 2 == 0:
-                o1[m // 2] = sb([P, 2, D], F32, "raw_z1" + str(m // 2))
-            for f in range(2):
-                bk = bank(group)
-                for g in range(2):
-                    nc.tensor.matmul_mx(
-                        out=bk[:],
-                        lhsT=r_c[:, g * 1024 + m * P : g * 1024 + (m + 1) * P].bitcast(E5),
-                        lhsT_scale=r_s[:, g * 1024 + m * P : g * 1024 + (m + 1) * P],
-                        rhs=q_c[:, g * 1024 + f * N : g * 1024 + (f + 1) * N].bitcast(E4),
-                        rhs_scale=q_s[:, g * 1024 + f * N : g * 1024 + (f + 1) * N],
-                        start=(g == 0),
-                        stop=(g == 1),
-                    )
-                scaled_out(engs[f], o1[m // 2][:, m % 2, f * N : (f + 1) * N], bk[:])
-            nc.sync.dma_start(out=out_1[m * P : (m + 1) * P, :], in_=o1[m // 2][:, m % 2, :])
-
-        load_v(0)
-        load_v(1)
-        load_g(0)
-        load_z2(0)
-        load_k(0)
-        load_z1(0, 0)
-        load_g(1)
-        load_z2(1)
-        load_v(2)
-        load_v(3)
-        load_k(1)
-        load_z1(0, 1)
-
-        for b in range(4):
-            v_block(b, "S")
-        v_quant(0)
-
-        def half_n0(h, extra):
-            for b in range(4 * h, 4 * h + 4):
-                mask_g(b)
-                dz2_t(b)
-                dl_mm(b, 0)
-                mask_dl(b, 0)
-                if b % 2:
-                    dz1_t(b // 2, 0)
-                extra(b)
-
-        def extra0(b):
-            if b < 2:
-                kq_half("k", 0, b, "VS")
             else:
-                for i in range(2):
-                    v_block(2 * b + i, "S")
+                m = x[0]
+                nc.sync.dma_start(out=out_1[m * P : (m + 1) * P, :], in_=o1[m // 2][:, m % 2, :])
 
-        half_n0(0, extra0)
-        load_g(2)
-        load_z2(2)
-        load_z1(1, 0)
-        load_g(3)
-        v_quant(1)
-        load_z2(3)
-        load_q(0)
-        load_q(1)
-        load_z1(1, 1)
-        for b in range(4):
-            dl_mm(b, 1)
-            mask_dl(b, 1)
-            if b % 2:
-                dz1_t(b // 2, 1)
-            if b < 2:
-                kq_half("k", 1, b, "VS")
-        r_quad(0, 0, "VS")
-        r_quad(0, 1, "VS")
-
-        def extra1(b):
-            out0_block(b - 4, "SS")
-
-        half_n0(1, extra1)
-        for h in range(2):
-            for half in range(2):
-                kq_half("q", h, half, "VS")
-        r_quad(1, 0, "VS")
-        for b in range(4, 8):
-            dl_mm(b, 1)
-            mask_dl(b, 1)
-            if b % 2:
-                dz1_t(b // 2, 1)
-            out1_block(b - 4, "SV", "O")
-        r_quad(1, 1, "VS")
-        for b in range(4, 8):
-            out0_block(b, "SV", "O")
-        for m in range(4, 8):
-            out1_block(m, "SV", "all")
+        with tc.manual_schedule():
+            for item in ORDER:
+                parts = item.split(":")
+                op(parts[0], parts[-1])

@@ -22,18 +22,18 @@ N = 512
 SCALE = 1.0 / 32.0
 
 ORDER = (
-    "vp0 vp2 vp3 vT0 vp1 vT1 vC0:V vT5 g1 vC1:S vT4 vC5:V vT6 z21 vC4:S vT7 vC6:V vT3 vC7:S vT2 vC3:S vQ10:V g0 "
-    "vC2:V z20 vQ00:V vQ01:V A2:V kp0 vQ11:V B2 A3:V C2:S D2:V B3 A0:V z100 E20 C3:S E21 A1:V B0 D3:V kp1 B1 C0:V "
-    "E30 kI000:V C1:S D0:V kI001:S D1:V F20:V E10 z101 kI011:S F30:V E00 kQ00:V kI010:S G10 F00:V E01 kI100:S "
-    "kI101:V g3 E31 F10:V E11 H10:S kQ01:V z23 kI110:S G00 kQ10:V F31:V H00:S F01:V kI111:S F21:V qp0 dI001:S F11:V "
-    "G11 I00:V dI000:S G01 kQ11:V A6:V H01:S z22 H11:S I01:V dI010:S B6 dQ00:V J01 I11:V C6:S qI011:V g2 J11 qI001:S "
-    "I10:V J10 D6:V z110 A7:V J31 qI000:S J30 K31:S dI011:V J00 K10:S qQ00:V J21 qI010:S J20 z111 A4:V E60 K00:S "
-    "A5:V B7 K21:S B4 C7:S qQ01:V qp1 B5 C4:S D7:V E61 F60:V C5:S E70 D4:V K01:S D5:V E40 K11:S F70:V E51 K30:S "
-    "F40:V E50 K20:S F51:V so0 E41 F50:V E71 F41:V dI100:S G20 F71:V G21 F61:V H20:S so1 G30 H21:S G31 I20:V qI110:S "
-    "I21:V H31:V J40 H30:S qI101:V J50 K40:S I30:V J41 I31:V K50:S dI101:V J51 K41:S J60 qI100:V K51:S J61 dQ10:V "
-    "qI111:S J71 qQ10:V J70 K60:V so2 K71:S O10 K61:V K70:S O20 qQ11:V dI111:S O00 P20:V O21 so3 dI110:V O31 P21:S "
-    "dQ01:V O30 P00:S dQ11:V O01 P30:S P31:V O11 sp2 P10:S O51 P01:V O71 P11:V sp3 P51:S O41 P71:S O40 sp0 P41:V O70 "
-    "P40:V O61 sp1 P70:V O60 P61:S O50 sp4 P60:S P50:V sp7 sp5 sp6 "
+    "vp2 vp1 vp0 vT4 g0 vT5 vC4:V vT3 vC5:S z2b1 vT2 vC3:V vT0 vC2:V vp3 vT1 vC0:V vC1:V z2b0 vQ01:V z2b3 A1:V vT7 "
+    "g1 vQ00:V vT6 vC7:S B1 A0:V vC6:S z2b2 C1:S vQ10:V B0 kp1 D1:V C0:S E10 A3:V vQ11:V B3 z101 A2:V E11 C3:S D0:V "
+    "B2 D3:V kI110:S kI111:V E01 kp0 E31 C2:S kQ11:V E30 kI100:S D2:V F11:V E21 z1000 kI101:S F01:V E00 F21:V G01 "
+    "z1001 F31:V E20 kI011:S kI010:V z23 G11 kQ10:V kI001:S F00:V F10:V kI000:S F20:V g3 G00 F30:V H01:S kQ00:V z22 "
+    "G10 H00:S I01:V H11:S I00:V kQ01:V H10:S J10 dI010:S J01 A7:V g2 J00 K01:S I10:V B7 qp0 I11:V K10:S A6:V J20 "
+    "dI011:S J30 dI001:V B6 K20:S A5:V z111 J31 K00:S J11 C7:S A4:V B5 C6:S K30:S dI000:V B4 qp1 C5:S D6:V J21 D7:V "
+    "qI010:S C4:V E70 D5:V E61 qI011:V K11:S z110 E60 D4:V K31:S E51 F61:V qI000:S E41 qI001:V E71 F51:V K21:S so1 "
+    "E40 F41:V qI101:S E50 F71:V so0 G21 qI100:V qI111:S G31 F50:V so3 F40:V H31:S F70:V H21:S G20 so2 F60:V H20:S "
+    "I31:V G30 I21:V dI101:S I20:V dQ00:V J41 H30:S qQ00:V J40 K41:S qQ10:V J51 K40:S J50 I30:V qQ01:V K51:S J70 "
+    "dI100:V K50:S J71 so4 qI110:V J60 K70:S dQ10:V J61 K71:S so5 qQ11:V K60:S O20 K61:V O21 so7 P20:S dI111:V O31 "
+    "P21:S dI110:V O30 so6 P31:S O10 dQ11:V P30:S O11 sp2 dQ01:V O01 P10:V P11:S O00 sp3 P01:V O51 P00:V O50 sp1 "
+    "P51:S O70 P50:S O71 P70:V sp0 O41 P71:V O40 P41:V sp5 O60 P40:V O61 P60:V sp7 P61:V sp4 sp6 "
 ).split()
 
 
@@ -168,14 +168,21 @@ def tile_scaledconvolutionaldotproduct_pa_v_kernel(tc, qp, kp, vp, mask, z1, z2,
                 i = x[0]
                 raw["g", i] = sb([P, 2, D], BF16, take("raw_g", name))
                 load(raw["g", i][:], g4[i // 2, :, 2 * (i % 2) : 2 * (i % 2) + 2, :])
+            elif k == "zb":
+                b = x[1]
+                if ("z2", b // 2) not in raw:
+                    raw["z2", b // 2] = sb([P, 2, D], F32, "raw_z2" + str(b // 2))
+                load(raw["z2", b // 2][:, b % 2, :], z24[b // 4, :, b % 4, :])
             elif k == "z" and x[0] == 2:
                 i = x[1]
                 raw["z2", i] = sb([P, 2, D], F32, "raw_z2" + str(i))
                 load(raw["z2", i][:], z24[i // 2, :, 2 * (i % 2) : 2 * (i % 2) + 2, :])
             elif k == "z":
                 h, n = x[1], x[2]
-                raw["z1", h, n] = sb([P, 4, N], F32, "raw_z1" + str(2 * h + n))
-                load(raw["z1", h, n][:], z14[h, :, :, n * N : (n + 1) * N])
+                js = range(2 * x[3], 2 * x[3] + 2) if len(x) == 4 else range(4)
+                if ("z1", h, n) not in raw:
+                    raw["z1", h, n] = sb([P, 4, N], F32, "raw_z1" + str(2 * h + n))
+                load(raw["z1", h, n][:, js[0] : js[-1] + 1, :], z14[h, :, js[0] : js[-1] + 1, n * N : (n + 1) * N])
             elif k == "kp":
                 raw["k", x[0]] = sb([P, 4, D], BF16, "raw_k" + str(x[0]))
                 load(raw["k", x[0]][:], kp4[x[0]])
@@ -245,7 +252,13 @@ def tile_scaledconvolutionaldotproduct_pa_v_kernel(tc, qp, kp, vp, mask, z1, z2,
             elif k in ("kI", "qI", "dI"):
                 h, f, i = x
                 if (c, h, f) not in grp4:
-                    grp4[c, h, f] = sb([P, 2048], BF16, take("grp", (c, h, f)))
+                    if c == "q":
+                        if ("qt", h) not in grp4:
+                            grp4["qt", h] = sb([P, 4096], BF16, "raw_k" + str(h))
+                        grp4[c, h, f] = grp4["qt", h][:, f * 2048 : (f + 1) * 2048]
+                    else:
+                        new = sb([P, 2048], BF16, take("grp", (c, h, f)))
+                        grp4[c, h, f] = new[:]
                 if c == "d":
                     src = dz1[h, f][:].rearrange("p (t c) -> p t c", t=4)[:, :, i * 256 : (i + 1) * 256]
                 else:
@@ -258,8 +271,9 @@ def tile_scaledconvolutionaldotproduct_pa_v_kernel(tc, qp, kp, vp, mask, z1, z2,
             elif k in ("kQ", "qQ", "dQ"):
                 h, f = x
                 cc, ss, dt = {"k": (k_c, k_s, E4), "q": (q_c, q_s, E4), "d": (r_c, r_s, E5)}[c]
-                quant(cc, ss, dt, grp4[c, h, f][:], h * 1024 + f * N, N)
-                give((c, h, f))
+                quant(cc, ss, dt, grp4[c, h, f], h * 1024 + f * N, N)
+                if c != "q":
+                    give((c, h, f))
             elif k == "J":
                 b, f = x
                 product(name, d_c, d_s, [g * 1024 + b * P for g in range(2)], k_c, k_s, [g * 1024 + f * N for g in range(2)])
@@ -277,8 +291,8 @@ def tile_scaledconvolutionaldotproduct_pa_v_kernel(tc, qp, kp, vp, mask, z1, z2,
                     o1[m // 2] = sb([P, 2, D], F32, "raw_z1" + str(m // 2))
                 scaled_out(eng, o1[m // 2][:, m % 2, f * N : (f + 1) * N], drain("O" + str(m) + str(f))[:])
             elif k == "so":
-                i = x[0]
-                nc.sync.dma_start(out=out04[i // 2, :, 2 * (i % 2) : 2 * (i % 2) + 2, :], in_=o0[i][:])
+                b = x[0]
+                nc.sync.dma_start(out=out04[b // 4, :, b % 4, :], in_=o0[b // 2][:, b % 2, :])
             else:
                 m = x[0]
                 nc.sync.dma_start(out=out_1[m * P : (m + 1) * P, :], in_=o1[m // 2][:, m % 2, :])

@@ -22,18 +22,18 @@ N = 512
 SCALE = 1.0 / 32.0
 
 ORDER = (
-    "vp2 vp1 vp0 vT4 g0 vT5 vC4:V vT3 vC5:S z2b1 vT2 vC3:V vT0 vC2:V vp3 vT1 vC0:V vC1:V z2b0 vQ01:V z2b3 A1:V vT7 "
-    "g1 vQ00:V vT6 vC7:S B1 A0:V vC6:S z2b2 C1:S vQ10:V B0 kp1 D1:V C0:S E10 A3:V vQ11:V B3 z101 A2:V E11 C3:S D0:V "
-    "B2 D3:V kI110:S kI111:V E01 kp0 E31 C2:S kQ11:V E30 kI100:S D2:V F11:V E21 z1000 kI101:S F01:V E00 F21:V G01 "
-    "z1001 F31:V E20 kI011:S kI010:V z23 G11 kQ10:V kI001:S F00:V F10:V kI000:S F20:V g3 G00 F30:V H01:S kQ00:V z22 "
-    "G10 H00:S I01:V H11:S I00:V kQ01:V H10:S J10 dI010:S J01 A7:V g2 J00 K01:S I10:V B7 qp0 I11:V K10:S A6:V J20 "
-    "dI011:S J30 dI001:V B6 K20:S A5:V z111 J31 K00:S J11 C7:S A4:V B5 C6:S K30:S dI000:V B4 qp1 C5:S D6:V J21 D7:V "
-    "qI010:S C4:V E70 D5:V E61 qI011:V K11:S z110 E60 D4:V K31:S E51 F61:V qI000:S E41 qI001:V E71 F51:V K21:S so1 "
-    "E40 F41:V qI101:S E50 F71:V so0 G21 qI100:V qI111:S G31 F50:V so3 F40:V H31:S F70:V H21:S G20 so2 F60:V H20:S "
-    "I31:V G30 I21:V dI101:S I20:V dQ00:V J41 H30:S qQ00:V J40 K41:S qQ10:V J51 K40:S J50 I30:V qQ01:V K51:S J70 "
-    "dI100:V K50:S J71 so4 qI110:V J60 K70:S dQ10:V J61 K71:S so5 qQ11:V K60:S O20 K61:V O21 so7 P20:S dI111:V O31 "
-    "P21:S dI110:V O30 so6 P31:S O10 dQ11:V P30:S O11 sp2 dQ01:V O01 P10:V P11:S O00 sp3 P01:V O51 P00:V O50 sp1 "
-    "P51:S O70 P50:S O71 P70:V sp0 O41 P71:V O40 P41:V sp5 O60 P40:V O61 P60:V sp7 P61:V sp4 sp6 "
+    "vp0 vp1 g0 vT1 vp3 vT0 vC1:S vT2 z2b0 vT3 vC2:S vC0:S vp2 vC3:S vT7 z2b1 vQ01:V vT6 vC7:S A0:V g1 vC6:V vT4 "
+    "z2b3 vT5 vQ00:V B0 A1:V vC5:S z2b2 C0:S B1 vC4:S D0:V kp1 E00 C1:S A3:V A2:V B3 z10 C3:S vQ10:V B2 vQ11:V C2:S "
+    "D1:V kp0 D3:V kI110:S E11 kI111:V E10 D2:V kI101:S E01 kQ11:V E31 F11:V z11 E30 kI100:S F01:V E20 F10:V G01 "
+    "F00:V kI010:S z23 kI011:V G00 kQ10:V E21 H01:S kQ01:V H00:S I01:V kI001:S F21:V g3 I00:V F31:V kI000:S J11 z22 "
+    "F20:V J01 F30:V dI010:S G11 kQ00:V G10 H11:S A7:V g2 J00 H10:S J10 A6:V K01:S qp0 B7 K10:S I11:V K11:S B6 I10:V "
+    "dI000:V K00:S J30 z12 C7:S A4:V J21 dI011:S J20 A5:V B4 C6:S J31 z13 qI011:V C4:S B5 D7:V K21:S D6:V E71 C5:S "
+    "D4:V dI001:V E60 K31:S qp1 E40 D5:V K20:S dQ00:V E50 qI000:S F40:V E51 F50:V E41 K30:S F51:V E61 so0 qI010:S "
+    "F41:V G20 F61:V so2 G21 H20:S F71:V E70 H21:S so1 F60:V G31 qI111:S I20:V F70:V so3 I21:V qI110:S G30 qQ01:V "
+    "J40 qI100:V H30:S J50 H31:V dI101:S J51 dI100:V J41 I31:V K40:S I30:V qI101:V K41:S J70 qQ11:V K50:S J71 J61 "
+    "dQ10:V K51:S so4 J60 K70:S qI001:V O01 K71:S qQ10:V so5 O21 K60:S qQ00:V K61:S dQ01:V so7 O20 P21:S P01:V O00 "
+    "P20:S dI111:V O31 so6 P00:S O30 dI110:V P31:S O10 sp2 dQ11:V O11 P10:S P30:V O50 sp0 P11:V O70 P50:S O51 sp3 "
+    "P70:S O41 P51:V O71 sp1 P41:V O60 P71:V O40 sp5 P60:V O61 P40:V sp7 P61:V sp4 sp6 "
 ).split()
 
 
@@ -44,8 +44,7 @@ def tile_scaledconvolutionaldotproduct_pa_v_kernel(tc, qp, kp, vp, mask, z1, z2,
     def by_four(a):
         return a.rearrange("(h p j) w -> h p j w", p=P, j=4)
 
-    qp4, kp4, z14, z24, g4, out04 = [by_four(a) for a in (qp, kp, z1, z2, grad_out, out_0)]
-    vp_rows = vp.rearrange("(b p) w -> p b w", p=P)
+    qp4, kp4, vp4, z14, z24, g4, out04 = [by_four(a) for a in (qp, kp, vp, z1, z2, grad_out, out_0)]
 
     with ExitStack() as ctx:
         keep = ctx.enter_context(tc.tile_pool(name="keep", bufs=1))
@@ -163,7 +162,7 @@ def tile_scaledconvolutionaldotproduct_pa_v_kernel(tc, qp, kp, vp, mask, z1, z2,
                 i = x[0]
                 if ("v", i // 2) not in raw:
                     raw["v", i // 2] = sb([P, 4, D], BF16, "raw_v" + str(i // 2))
-                load(raw["v", i // 2][:, 2 * (i % 2) : 2 * (i % 2) + 2, :], vp_rows[:, 2 * i : 2 * i + 2, :])
+                load(raw["v", i // 2][:, 2 * (i % 2) : 2 * (i % 2) + 2, :], vp4[i // 2, :, 2 * (i % 2) : 2 * (i % 2) + 2, :])
             elif k == "g":
                 i = x[0]
                 raw["g", i] = sb([P, 2, D], BF16, take("raw_g", name))
@@ -178,11 +177,9 @@ def tile_scaledconvolutionaldotproduct_pa_v_kernel(tc, qp, kp, vp, mask, z1, z2,
                 raw["z2", i] = sb([P, 2, D], F32, "raw_z2" + str(i))
                 load(raw["z2", i][:], z24[i // 2, :, 2 * (i % 2) : 2 * (i % 2) + 2, :])
             elif k == "z":
-                h, n = x[1], x[2]
-                js = range(2 * x[3], 2 * x[3] + 2) if len(x) == 4 else range(4)
-                if ("z1", h, n) not in raw:
-                    raw["z1", h, n] = sb([P, 4, N], F32, "raw_z1" + str(2 * h + n))
-                load(raw["z1", h, n][:, js[0] : js[-1] + 1, :], z14[h, :, js[0] : js[-1] + 1, n * N : (n + 1) * N])
+                i = x[1]
+                raw["z1", i] = sb([P, 2, D], F32, "raw_z1" + str(i))
+                load(raw["z1", i][:], z14[i // 2, :, 2 * (i % 2) : 2 * (i % 2) + 2, :])
             elif k == "kp":
                 raw["k", x[0]] = sb([P, 4, D], BF16, "raw_k" + str(x[0]))
                 load(raw["k", x[0]][:], kp4[x[0]])
@@ -230,10 +227,10 @@ def tile_scaledconvolutionaldotproduct_pa_v_kernel(tc, qp, kp, vp, mask, z1, z2,
                 if (h, n) not in dz1:
                     dz1[h, n] = sb([P, 4 * N], BF16, "dz1_" + str(2 * h + n))
                 nc.vector.scalar_tensor_tensor(
-                    out=dz1[h, n][:, j * N : (j + 1) * N],
-                    in0=raw["z1", h, n][:, j, :],
+                    out=dz1[h, n][:, j * N : (j + 1) * N].rearrange("p (w i) -> p w i", i=4),
+                    in0=raw["z1", b // 2][:, b % 2, n * N : (n + 1) * N].rearrange("p (w i) -> p w i", i=4),
                     scalar=0.0,
-                    in1=drain("E" + str(b) + str(n))[:],
+                    in1=drain("E" + str(b) + str(n))[:].rearrange("p (i w) -> p w i", i=4),
                     op0=ALU.is_gt,
                     op1=ALU.mult,
                 )

@@ -22,18 +22,18 @@ N = 512
 SCALE = 1.0 / 32.0
 
 ORDER = (
-    "vp0 vp1 g0 vT1 vp3 vT0 vC1:S vT2 z2b0 vT3 vC2:S vC0:S vp2 vC3:S vT7 z2b1 vQ01:V vT6 vC7:S A0:V g1 vC6:V vT4 "
-    "z2b3 vT5 vQ00:V B0 A1:V vC5:S z2b2 C0:S B1 vC4:S D0:V kp1 E00 C1:S A3:V A2:V B3 z10 C3:S vQ10:V B2 vQ11:V C2:S "
-    "D1:V kp0 D3:V kI110:S E11 kI111:V E10 D2:V kI101:S E01 kQ11:V E31 F11:V z11 E30 kI100:S F01:V E20 F10:V G01 "
-    "F00:V kI010:S z23 kI011:V G00 kQ10:V E21 H01:S kQ01:V H00:S I01:V kI001:S F21:V g3 I00:V F31:V kI000:S J11 z22 "
-    "F20:V J01 F30:V dI010:S G11 kQ00:V G10 H11:S A7:V g2 J00 H10:S J10 A6:V K01:S qp0 B7 K10:S I11:V K11:S B6 I10:V "
-    "dI000:V K00:S J30 z12 C7:S A4:V J21 dI011:S J20 A5:V B4 C6:S J31 z13 qI011:V C4:S B5 D7:V K21:S D6:V E71 C5:S "
-    "D4:V dI001:V E60 K31:S qp1 E40 D5:V K20:S dQ00:V E50 qI000:S F40:V E51 F50:V E41 K30:S F51:V E61 so0 qI010:S "
-    "F41:V G20 F61:V so2 G21 H20:S F71:V E70 H21:S so1 F60:V G31 qI111:S I20:V F70:V so3 I21:V qI110:S G30 qQ01:V "
-    "J40 qI100:V H30:S J50 H31:V dI101:S J51 dI100:V J41 I31:V K40:S I30:V qI101:V K41:S J70 qQ11:V K50:S J71 J61 "
-    "dQ10:V K51:S so4 J60 K70:S qI001:V O01 K71:S qQ10:V so5 O21 K60:S qQ00:V K61:S dQ01:V so7 O20 P21:S P01:V O00 "
-    "P20:S dI111:V O31 so6 P00:S O30 dI110:V P31:S O10 sp2 dQ11:V O11 P10:S P30:V O50 sp0 P11:V O70 P50:S O51 sp3 "
-    "P70:S O41 P51:V O71 sp1 P41:V O60 P71:V O40 sp5 P60:V O61 P40:V sp7 P61:V sp4 sp6 "
+    "vp0 vp1 g0 vT0 z2b0 vT1 vC0:S vT2 z2b1 vC1:S vT3 vC2:V vp2 vC3:S A0:V vp3 A1:V B0 z2b2 vQ01:V vT4 g1 B1 vC4:S "
+    "vT5 z2b3 C1:V C0:S vT6 vQ00:V vT7 vC6:S kp0 D1:V D0:V vC7:S E00 A2:V vC5:S E10 vQ10:V B2 z10 vQ11:V A3:V E01 "
+    "kI010:S C2:V kI011:G kp1 B3 C3:S D2:V kI001:S kI000:G E20 F10:V z11 E21 F00:V D3:V G00 F01:V E30 kQ01:V H00:S "
+    "z22 E11 kQ00:V kI101:S E31 I00:V F11:V kI111:G kI100:S G01 F21:V g2 F31:V kI110:G H01:S F30:V z23 G11 dI011:S "
+    "F20:V kQ10:V G10 dI000:S I01:V kQ11:V J00 g3 H10:S A4:V J01 H11:S J11 qp0 A5:V dI001:S J10 B4 I11:V K11:S B5 "
+    "I10:V C4:S A6:V z13 J31 K01:S J21 A7:V K31:S J30 B6 D4:V qI000:S qp1 B7 K10:V qI001:G C5:V J20 C6:S E41 D5:V "
+    "K21:S E40 D6:V z12 C7:S dQ00:V E60 K30:S D7:V E61 qQ00:V K00:S E70 F60:V K20:S E71 qI110:G so3 F61:V qI011:S "
+    "E51 F70:V E50 so1 F71:V qI111:S qI010:G G30 G31 F41:V so0 H30:S F51:V qI101:G H31:S F40:V G21 so2 qI100:S F50:V "
+    "I31:V G20 I30:V H21:S dI101:V J60 H20:S dI100:V J61 K60:S J70 I20:V I21:V K61:S J71 qQ11:V K70:S J50 qQ10:V "
+    "K71:S J51 so6 dQ10:V K50:S J41 qQ01:V J40 K51:S so7 K41:V O00 dI010:S O01 K40:V so5 O11 dI110:V P00:S O10 "
+    "dI111:V P01:S so4 O20 P11:S dQ01:V O21 P10:S dQ11:V sp0 O31 P21:S P20:V O30 P31:V O40 sp1 P30:V O50 P40:S O51 "
+    "sp2 P50:V O41 P51:V O61 sp3 P41:V O70 P61:S O60 sp5 P70:S O71 P60:S sp4 P71:S sp6 sp7 "
 ).split()
 
 
@@ -94,7 +94,7 @@ def tile_scaledconvolutionaldotproduct_pa_v_kernel(tc, qp, kp, vp, mask, z1, z2,
             free_banks.append(tag)
             return tile
 
-        v_grp = {n: sb([P, 4096], BF16, "raw_z23" if n == 0 else "raw_z13") for n in range(2)}
+        v_grp = {n: sb([P, 4096], BF16, "raw_z23" if n == 0 else "raw_z12") for n in range(2)}
         raw = {}
         masked = []
         dz2 = {}
@@ -260,11 +260,22 @@ def tile_scaledconvolutionaldotproduct_pa_v_kernel(tc, qp, kp, vp, mask, z1, z2,
                     src = dz1[h, f][:].rearrange("p (t c) -> p t c", t=4)[:, :, i * 256 : (i + 1) * 256]
                 else:
                     src = raw[c, h][:, :, f * N + i * 256 : f * N + (i + 1) * 256]
-                copy_out(
-                    eng,
-                    grp4[c, h, f][:, i * 1024 : (i + 1) * 1024].rearrange("p (c i t) -> p c t i", i=4, t=4),
-                    src.rearrange("p t (c i) -> p c t i", i=4),
-                )
+                dst = grp4[c, h, f][:, i * 1024 : (i + 1) * 1024]
+                if eng == "G":
+                    nc.gpsimd.tensor_scalar(
+                        out=dst.rearrange("p (c t) -> p c t", t=4),
+                        in0=src.rearrange("p t c -> p c t"),
+                        scalar1=1.0,
+                        scalar2=0.0,
+                        op0=ALU.mult,
+                        op1=ALU.add,
+                    )
+                else:
+                    copy_out(
+                        eng,
+                        dst.rearrange("p (c i t) -> p c t i", i=4, t=4),
+                        src.rearrange("p t (c i) -> p c t i", i=4),
+                    )
             elif k in ("kQ", "qQ", "dQ"):
                 h, f = x
                 cc, ss, dt = {"k": (k_c, k_s, E4), "q": (q_c, q_s, E4), "d": (r_c, r_s, E5)}[c]

from contextlib import ExitStack

import concourse.mybir as mybir
from concourse.masks import make_identity

S = 1024
D = 1024
FLOPS = 3 * 2 * S * S * D
BYTES = 4 * S * D * 2 + 2 * S * D * 4 + 2 * S * D * 4

F32 = mybir.dt.float32
BF16 = mybir.dt.bfloat16
U32 = mybir.dt.uint32
U8 = mybir.dt.uint8
E4 = mybir.dt.float8_e4m3fn_x4
E5 = mybir.dt.float8_e5m2_x4
ALU = mybir.AluOpType
COPY = mybir.ActivationFunctionType.Copy

P = 128
N = 512
SCALE = 1.0 / 32.0

ORDER = (
    "vp0 vp1 g0 vT0 z2b0 vT1 vC0:S vT2 z2b1 vC1:S vT3 vC2:V vp2 vC3:S A0:V vp3 A1:V B0 z2b2 vQ01:V vT4 g1 B1 vC4:S "
    "vT5 z2b3 C1:V C0:S vT6 vQ00:V vT7 vC6:S kp0 D1:V D0:V vC7:S E00 A2:V vC5:S E10 vQ10:V B2 z10 vQ11:V A3:V E01 "
    "kI010:S C2:V kI011:G kp1 B3 C3:S D2:V kI001:S kI000:G E20 F10:V z11 E21 F00:V D3:V G00 F01:V E30 kQ01:V H00:S "
    "z22 E11 kQ00:V kI101:S E31 I00:V F11:V kI111:G kI100:S G01 F21:V g2 F31:V kI110:G H01:S F30:V z23 G11 dI011:S "
    "F20:V kQ10:V G10 dI000:S I01:V kQ11:V J00 g3 H10:S A4:V J01 H11:S J11 qp0 A5:V dI001:S J10 B4 I11:V K11:S B5 "
    "I10:V C4:S A6:V z13 J31 K01:S J21 A7:V K31:S J30 B6 D4:V qI000:S qp1 B7 K10:V qI001:G C5:V J20 C6:S E41 D5:V "
    "K21:S E40 D6:V z12 C7:S dQ00:V E60 K30:S D7:V E61 qQ00:V K00:S E70 F60:V K20:S E71 qI110:G so3 F61:V qI011:S "
    "E51 F70:V E50 so1 F71:V qI111:S qI010:G G30 G31 F41:V so0 H30:S F51:V qI101:G H31:S F40:V G21 so2 qI100:S F50:V "
    "I31:V G20 I30:V H21:S dI101:V J60 H20:S dI100:V J61 K60:S J70 I20:V I21:V K61:S J71 qQ11:V K70:S J50 qQ10:V "
    "K71:S J51 so6 dQ10:V K50:S J41 qQ01:V J40 K51:S so7 K41:V O00 dI010:S O01 K40:V so5 O11 dI110:V P00:S O10 "
    "dI111:V P01:S so4 O20 P11:S dQ01:V O21 P10:S dQ11:V sp0 O31 P21:S P20:V O30 P31:V O40 sp1 P30:V O50 P40:S O51 "
    "sp2 P50:V O41 P51:V O61 sp3 P41:V O70 P61:S O60 sp5 P70:S O71 P60:S sp4 P71:S sp6 sp7 "
).split()


def tile_scaledconvolutionaldotproduct_pa_v_kernel(tc, qp, kp, vp, mask, z1, z2, grad_out, out_0, out_1):
    nc = tc.nc
    qp, kp, vp, z1, z2, grad_out, out_0, out_1 = [a.flatten_outer_dims() for a in (qp, kp, vp, z1, z2, grad_out, out_0, out_1)]

    def by_four(a):
        return a.rearrange("(h p j) w -> h p j w", p=P, j=4)

    qp4, kp4, vp4, z14, z24, g4, out04 = [by_four(a) for a in (qp, kp, vp, z1, z2, grad_out, out_0)]

    with ExitStack() as ctx:
        keep = ctx.enter_context(tc.tile_pool(name="keep", bufs=1))
        psum = ctx.enter_context(tc.psum_pool(name="psum", bufs=1))

        ident = keep.tile([P, P], F32, name="ident")
        make_identity(nc, ident[:])

        def codes(name):
            c = keep.tile([P, 2048], U32, name=name + "_codes", align_bytes=64)
            s = keep.tile([P, 2048], U8, name=name + "_scales", align_bytes=64)
            return c, s

        v_c, v_s = codes("v")
        k_c, k_s = codes("k")
        q_c, q_s = codes("q")
        t_c, t_s = codes("t")
        d_c, d_s = codes("d")
        r_c, r_s = codes("r")

        def sb(shape, dt, tag):
            return keep.tile(shape, dt, tag=tag, name=tag, align_bytes=64)

        free_banks = ["bank" + str(i) for i in range(8)]
        bank_of = {}
        free_slots = {k: [k + str(i) for i in range(n)] for k, n in (("grp", 5), ("dz2_", 4), ("tg", 4), ("dg", 4), ("raw_g", 3))}
        slot_of = {}

        def take(kind, key):
            tag = free_slots[kind][0]
            free_slots[kind].remove(tag)
            slot_of[key] = (kind, tag)
            return tag

        def give(key):
            kind, tag = slot_of[key]
            free_slots[kind].append(tag)

        def bank(key):
            tag = free_banks[0]
            free_banks.remove(tag)
            bank_of[key] = (psum.tile([P, N], F32, tag=tag, name="bank"), tag)
            return bank_of[key][0]

        def drain(key):
            tile, tag = bank_of[key]
            free_banks.append(tag)
            return tile

        v_grp = {n: sb([P, 4096], BF16, "raw_z23" if n == 0 else "raw_z12") for n in range(2)}
        raw = {}
        masked = []
        dz2 = {}
        tg = {}
        dz1 = {}
        dg = {}
        grp4 = {}
        o0 = {}
        o1 = {}

        def load(out, src):
            nc.sync.dma_start(out=out, in_=src)

        def copy_out(eng, out, in_):
            if eng == "S":
                nc.scalar.copy(out=out, in_=in_)
            else:
                nc.vector.tensor_copy(out=out, in_=in_)

        def scaled_out(eng, out, in_):
            if eng == "S":
                nc.scalar.activation(out=out, in_=in_, func=COPY, scale=SCALE)
            else:
                nc.vector.tensor_scalar(out=out, in0=in_, scalar1=SCALE, scalar2=None, op0=ALU.mult)

        def transpose_words(key, blocks):
            b = bank(key)
            for i, w in enumerate(blocks):
                nc.tensor.transpose(b[:, i * P : (i + 1) * P], w, ident[:])

        def words(tile2d, start):
            w = tile2d.bitcast(F32)
            return [w[:, start + u : start + 256 : 2] for u in (0, 1)]

        def quant(out_c, out_s, dt, grp, at, width):
            nc.vector.quantize_mx(out=out_c[:, at : at + width].bitcast(dt), scales=out_s[:, at : at + width], in_=grp)

        def product(key, a_c, a_s, a_at, b_c, b_s, b_at):
            bk = bank(key)
            for g in range(2):
                a = slice(a_at[g], a_at[g] + P)
                b = slice(b_at[g], b_at[g] + N)
                nc.tensor.matmul_mx(
                    out=bk[:],
                    lhsT=a_c[:, a].bitcast(E5),
                    lhsT_scale=a_s[:, a],
                    rhs=b_c[:, b].bitcast(E4),
                    rhs_scale=b_s[:, b],
                    start=(g == 0),
                    stop=(g == 1),
                )

        def grouped(eng, out, bk):
            copy_out(
                eng,
                out.bitcast(F32).rearrange("p (g r u) -> p g r u", g=2, u=2),
                bk.rearrange("p (g u r) -> p g r u", g=2, u=2),
            )

        def op(name, eng):
            c = name[0]
            x = [int(ch) for ch in name if ch in "0123456789"]
            k = "".join([ch for ch in name if ch not in "0123456789"])
            if k == "vp":
                i = x[0]
                if ("v", i // 2) not in raw:
                    raw["v", i // 2] = sb([P, 4, D], BF16, "raw_v" + str(i // 2))
                load(raw["v", i // 2][:, 2 * (i % 2) : 2 * (i % 2) + 2, :], vp4[i // 2, :, 2 * (i % 2) : 2 * (i % 2) + 2, :])
            elif k == "g":
                i = x[0]
                raw["g", i] = sb([P, 2, D], BF16, take("raw_g", name))
                load(raw["g", i][:], g4[i // 2, :, 2 * (i % 2) : 2 * (i % 2) + 2, :])
            elif k == "zb":
                b = x[1]
                if ("z2", b // 2) not in raw:
                    raw["z2", b // 2] = sb([P, 2, D], F32, "raw_z2" + str(b // 2))
                load(raw["z2", b // 2][:, b % 2, :], z24[b // 4, :, b % 4, :])
            elif k == "z" and x[0] == 2:
                i = x[1]
                raw["z2", i] = sb([P, 2, D], F32, "raw_z2" + str(i))
                load(raw["z2", i][:], z24[i // 2, :, 2 * (i % 2) : 2 * (i % 2) + 2, :])
            elif k == "z":
                i = x[1]
                raw["z1", i] = sb([P, 2, D], F32, "raw_z1" + str(i))
                load(raw["z1", i][:], z14[i // 2, :, 2 * (i % 2) : 2 * (i % 2) + 2, :])
            elif k == "kp":
                raw["k", x[0]] = sb([P, 4, D], BF16, "raw_k" + str(x[0]))
                load(raw["k", x[0]][:], kp4[x[0]])
            elif k == "qp":
                raw["q", x[0]] = sb([P, 4, D], BF16, "raw_v" + str(x[0]))
                load(raw["q", x[0]][:], qp4[x[0]])
            elif k == "vT":
                row = raw["v", x[0] // 4][:, x[0] % 4, :]
                transpose_words(name, words(row, 0) + words(row, 256))
            elif k == "vC":
                n, i = x[0] // 4, x[0] % 4
                copy_out(
                    eng,
                    v_grp[n][:].bitcast(F32).rearrange("p (g r u) -> p g r u", g=2, u=2)[:, :, i * P : (i + 1) * P, :],
                    drain("vT" + str(x[0]))[:].rearrange("p (g u r) -> p g r u", g=2, u=2),
                )
            elif k == "vQ":
                n, g = x
                quant(v_c, v_s, E4, v_grp[n][:, g * 2048 : (g + 1) * 2048], (2 * n + g) * N, N)
            elif k == "A":
                b = x[0]
                dz2[b] = sb([P, D], BF16, take("dz2_", name))
                nc.vector.scalar_tensor_tensor(
                    out=dz2[b][:], in0=raw["z2", b // 2][:, b % 2, :], scalar=0.0, in1=raw["g", b // 2][:, b % 2, :], op0=ALU.is_gt, op1=ALU.mult
                )
                masked.append(b)
                if b ^ 1 in masked:
                    give("g" + str(b // 2))
            elif k == "B":
                transpose_words(name, words(dz2[x[0]][:], 0) + words(dz2[x[0]][:], 256))
                give("A" + str(x[0]))
            elif k == "C":
                b = x[0]
                tg[b] = sb([P, 1024], BF16, take("tg", name))
                grouped(eng, tg[b][:], drain("B" + str(b))[:])
            elif k == "D":
                quant(t_c, t_s, E5, tg[x[0]][:], x[0] * 256, 256)
                give("C" + str(x[0]))
            elif k == "E":
                b, n = x
                product(name, t_c, t_s, [b * 256 + g * P for g in range(2)], v_c, v_s, [(2 * n + g) * N for g in range(2)])
            elif k == "F":
                b, n = x
                h, j = b // 4, b % 4
                if (h, n) not in dz1:
                    dz1[h, n] = sb([P, 4 * N], BF16, "dz1_" + str(2 * h + n))
                nc.vector.scalar_tensor_tensor(
                    out=dz1[h, n][:, j * N : (j + 1) * N].rearrange("p (w i) -> p w i", i=4),
                    in0=raw["z1", b // 2][:, b % 2, n * N : (n + 1) * N].rearrange("p (w i) -> p w i", i=4),
                    scalar=0.0,
                    in1=drain("E" + str(b) + str(n))[:].rearrange("p (i w) -> p w i", i=4),
                    op0=ALU.is_gt,
                    op1=ALU.mult,
                )
            elif k == "G":
                p, n = x
                h, j = p // 2, 2 * (p % 2)
                transpose_words(name, words(dz1[h, n][:], j * 256) + words(dz1[h, n][:], (j + 1) * 256))
            elif k == "H":
                p, n = x
                dg[p, n] = sb([P, 1024], BF16, take("dg", name))
                grouped(eng, dg[p, n][:], drain("G" + str(p) + str(n))[:])
            elif k == "I":
                p, n = x
                quant(d_c, d_s, E5, dg[p, n][:], n * 1024 + p * 256, 256)
                give("H" + str(p) + str(n))
            elif k in ("kI", "qI", "dI"):
                h, f, i = x
                if (c, h, f) not in grp4:
                    if c == "q":
                        if ("qt", h) not in grp4:
                            grp4["qt", h] = sb([P, 4096], BF16, "raw_k" + str(h))
                        grp4[c, h, f] = grp4["qt", h][:, f * 2048 : (f + 1) * 2048]
                    else:
                        new = sb([P, 2048], BF16, take("grp", (c, h, f)))
                        grp4[c, h, f] = new[:]
                if c == "d":
                    src = dz1[h, f][:].rearrange("p (t c) -> p t c", t=4)[:, :, i * 256 : (i + 1) * 256]
                else:
                    src = raw[c, h][:, :, f * N + i * 256 : f * N + (i + 1) * 256]
                dst = grp4[c, h, f][:, i * 1024 : (i + 1) * 1024]
                if eng == "G":
                    nc.gpsimd.tensor_scalar(
                        out=dst.rearrange("p (c t) -> p c t", t=4),
                        in0=src.rearrange("p t c -> p c t"),
                        scalar1=1.0,
                        scalar2=0.0,
                        op0=ALU.mult,
                        op1=ALU.add,
                    )
                else:
                    copy_out(
                        eng,
                        dst.rearrange("p (c i t) -> p c t i", i=4, t=4),
                        src.rearrange("p t (c i) -> p c t i", i=4),
                    )
            elif k in ("kQ", "qQ", "dQ"):
                h, f = x
                cc, ss, dt = {"k": (k_c, k_s, E4), "q": (q_c, q_s, E4), "d": (r_c, r_s, E5)}[c]
                quant(cc, ss, dt, grp4[c, h, f], h * 1024 + f * N, N)
                if c != "q":
                    give((c, h, f))
            elif k == "J":
                b, f = x
                product(name, d_c, d_s, [g * 1024 + b * P for g in range(2)], k_c, k_s, [g * 1024 + f * N for g in range(2)])
            elif k == "K":
                b, f = x
                if b // 2 not in o0:
                    o0[b // 2] = sb([P, 2, D], F32, "raw_z2" + str(b // 2))
                scaled_out(eng, o0[b // 2][:, b % 2, f * N : (f + 1) * N], drain("J" + str(b) + str(f))[:])
            elif k == "O":
                m, f = x
                product(name, r_c, r_s, [g * 1024 + m * P for g in range(2)], q_c, q_s, [g * 1024 + f * N for g in range(2)])
            elif k == "P":
                m, f = x
                if m // 2 not in o1:
                    o1[m // 2] = sb([P, 2, D], F32, "raw_z1" + str(m // 2))
                scaled_out(eng, o1[m // 2][:, m % 2, f * N : (f + 1) * N], drain("O" + str(m) + str(f))[:])
            elif k == "so":
                b = x[0]
                nc.sync.dma_start(out=out04[b // 4, :, b % 4, :], in_=o0[b // 2][:, b % 2, :])
            else:
                m = x[0]
                nc.sync.dma_start(out=out_1[m * P : (m + 1) * P, :], in_=o1[m // 2][:, m % 2, :])

        with tc.manual_schedule():
            for item in ORDER:
                parts = item.split(":")
                op(parts[0], parts[-1])
